import numpy as np
import ml_dtypes

BF16 = ml_dtypes.bfloat16


def bf(x):
    return np.asarray(x, np.float32).astype(BF16)


def f32(x):
    return np.asarray(x, np.float32)


def f64(x):
    return np.asarray(x).astype(np.float64)


def striped(idx):
    return np.tile(idx.reshape(-1, 16).T, (8, 1))


C, S, N = 256, 4096, 2048


def setup_inputs():
    return {
        "base": f32(np.random.standard_normal((C, S))),
        "pos": f32(np.random.standard_normal((C, S))),
        "tok": f32(0.5 * np.random.standard_normal((C, 1))),
        "prompt_table": bf(np.random.standard_normal((C, N))),
        "w1": bf(np.random.standard_normal((C, C)) / np.sqrt(C)),
        "b1": f32(0.5 * np.random.standard_normal((C, 1))),
        "w2": bf(np.random.standard_normal((C, C)) * np.sqrt(2.0 / C)),
        "b2": f32(0.5 * np.random.standard_normal((C, 1))),
        "offs": striped(np.random.permutation(S)[:N]),
    }


def reference(base, pos, tok, prompt_table, w1, b1, w2, b2, offs):
    idx = offs[:16].T.reshape(-1)
    h = np.maximum(f64(w1).T @ f64(prompt_table) + f64(b1), 0.0)
    y = f64(w2).T @ h
    raw = f64(base).copy()
    raw[:, idx] = y + f64(b2)
    return raw + f64(pos) + f64(tok)

@@ -1,0 +1,117 @@
+import concourse.mybir as mybir
+
+P = 128
+C, S, N = 256, 4096, 2048
+BLOCKS = C // P
+BANK = 512
+STORE = 1024
+
+FLOPS = 2 * 2 * C * C * N
+
+F32, BF16, U16 = mybir.dt.float32, mybir.dt.bfloat16, mybir.dt.uint16
+ALU = mybir.AluOpType
+ACT = mybir.ActivationFunctionType
+
+
+def block(b):
+    return slice(b * P, (b + 1) * P)
+
+
+def piece(i, width):
+    return slice(i * width, (i + 1) * width)
+
+
+def tile_pclembeddings_s_kernel(tc, base, pos, tok, prompt_table, w1, b1, w2, b2, offs, out):
+    nc = tc.nc
+    with (
+        tc.tile_pool(name="held", bufs=1) as held,
+        tc.psum_pool(name="psum_h", bufs=4) as psum_h,
+        tc.psum_pool(name="psum_y", bufs=2) as psum_y,
+    ):
+        offsets = held.tile([P, N // 16], U16, name="offsets")
+        blocks = range(BLOCKS)
+        w1_rows = [held.tile([P, C], BF16, name=f"w1_rows{b}") for b in blocks]
+        w2_rows = [held.tile([P, C], BF16, name=f"w2_rows{b}") for b in blocks]
+        table = [held.tile([P, N], BF16, name=f"table{b}") for b in blocks]
+        b1_cols = held.tile([P, BLOCKS], F32, name="b1_cols")
+        b2_cols = held.tile([P, BLOCKS], F32, name="b2_cols")
+        tok_cols = held.tile([P, BLOCKS], F32, name="tok_cols")
+        b2_wide = [held.tile([P, N], F32, name=f"b2_wide{b}") for b in blocks]
+        hidden = [held.tile([P, N], BF16, name=f"hidden{b}") for b in blocks]
+        y = [held.tile([P, N], F32, name=f"y{b}") for b in blocks]
+        window = [held.tile([P, S], F32, name=f"window{b}") for b in blocks]
+        total = [held.tile([P, S], F32, name=f"total{b}") for b in blocks]
+
+        nc.sync.dma_start(offsets[:], offs)
+        queues = [nc.sync, nc.scalar]
+        with nc.allow_non_contiguous_dma(reason="three bias vectors, one float32 to a partition"):
+            nc.sync.dma_start(b1_cols[:], b1.rearrange("(b p) o -> p (b o)", p=P))
+            nc.scalar.dma_start(b2_cols[:], b2.rearrange("(b p) o -> p (b o)", p=P))
+            nc.scalar.dma_start(tok_cols[:], tok.rearrange("(b p) o -> p (b o)", p=P))
+        for b in blocks:
+            queues[b].dma_start(w1_rows[b][:], w1[block(b), :])
+        for j in range(N // BANK):
+            for b in blocks:
+                queues[b].dma_start(table[b][:, piece(j, BANK)], prompt_table[block(b), piece(j, BANK)])
+        for b in blocks:
+            queues[b].dma_start(w2_rows[b][:], w2[block(b), :])
+        for tiles, array in ((window, base), (total, pos)):
+            for b in blocks:
+                for half in range(2):
+                    queues[half].dma_start(tiles[b][:, piece(half, S // 2)], array[block(b), piece(half, S // 2)])
+
+        for b in blocks:
+            nc.gpsimd.tensor_copy(b2_wide[b][:], b2_cols[:, b : b + 1].to_broadcast([P, N]))
+
+        def layer1(j):
+            cols = piece(j, BANK)
+            for ib in blocks:
+                acc_h = psum_h.tile([P, BANK], F32, name="acc_h")
+                for kb in blocks:
+                    nc.tensor.matmul(
+                        acc_h[:], w1_rows[kb][:, block(ib)], table[kb][:, cols],
+                        start=(kb == 0), stop=(kb == BLOCKS - 1),
+                    )
+                if ib == 0:
+                    nc.scalar.activation(hidden[ib][:, cols], acc_h[:], ACT.Relu, bias=b1_cols[:, ib : ib + 1])
+                else:
+                    nc.vector.tensor_scalar(hidden[ib][:, cols], acc_h[:], b1_cols[:, ib : ib + 1], 0.0, ALU.add, ALU.max)
+
+        def layer2(cb, j):
+            cols = piece(j, BANK)
+            acc_y = psum_y.tile([P, BANK], F32, name="acc_y")
+            for ib in blocks:
+                nc.tensor.matmul(
+                    acc_y[:], w2_rows[ib][:, block(cb)], hidden[ib][:, cols],
+                    start=(ib == 0), stop=(ib == BLOCKS - 1),
+                )
+            if cb == 0:
+                nc.vector.tensor_copy(y[cb][:, cols], acc_y[:])
+            else:
+                nc.scalar.copy(y[cb][:, cols], acc_y[:])
+
+        def scatter(cb):
+            nc.vector.tensor_tensor(window[cb][:].indirect(offsets[:]), y[cb][:], b2_wide[cb][:], ALU.add)
+
+        def finish(cb, engine):
+            for i in range(S // STORE):
+                cols = piece(i, STORE)
+                engine.tensor_tensor(total[cb][:, cols], window[cb][:, cols], total[cb][:, cols], ALU.add)
+                nc.sync.dma_start(out[block(cb), cols], total[cb][:, cols])
+
+        steps = N // BANK
+        layer1(0)
+        for j in range(1, steps):
+            layer1(j)
+            layer2(0, j - 1)
+        layer2(0, steps - 1)
+        scatter(0)
+        for j in range(steps):
+            layer2(1, j)
+        scatter(1)
+
+        for cb in blocks:
+            nc.scalar.activation(total[cb][:], total[cb][:], ACT.Identity, bias=tok_cols[:, cb : cb + 1])
+
+        finish(0, nc.gpsimd)
+        finish(1, nc.vector)

@@ -1,9 +1,11 @@
 import concourse.mybir as mybir
+from concourse.masks import make_identity
 
 P = 128
 C, S, N = 256, 4096, 2048
 BLOCKS = C // P
 BANK = 512
+BANKS = 8
 STORE = 1024
 
 FLOPS = 2 * 2 * C * C * N
@@ -23,95 +25,103 @@ def piece(i, width):
 
 def tile_pclembeddings_s_kernel(tc, base, pos, tok, prompt_table, w1, b1, w2, b2, offs, out):
     nc = tc.nc
-    with (
-        tc.tile_pool(name="held", bufs=1) as held,
-        tc.psum_pool(name="psum_h", bufs=4) as psum_h,
-        tc.psum_pool(name="psum_y", bufs=2) as psum_y,
-    ):
+    blocks = range(BLOCKS)
+    with tc.tile_pool(name="held", bufs=1) as held:
         offsets = held.tile([P, N // 16], U16, name="offsets")
-        blocks = range(BLOCKS)
-        w1_rows = [held.tile([P, C], BF16, name=f"w1_rows{b}") for b in blocks]
-        w2_rows = [held.tile([P, C], BF16, name=f"w2_rows{b}") for b in blocks]
+        w1_rows = held.tile([P, BLOCKS, C], BF16, name="w1_rows")
+        w2_rows = held.tile([P, BLOCKS, C], BF16, name="w2_rows")
         table = [held.tile([P, N], BF16, name=f"table{b}") for b in blocks]
         b1_cols = held.tile([P, BLOCKS], F32, name="b1_cols")
         b2_cols = held.tile([P, BLOCKS], F32, name="b2_cols")
         tok_cols = held.tile([P, BLOCKS], F32, name="tok_cols")
         b2_wide = [held.tile([P, N], F32, name=f"b2_wide{b}") for b in blocks]
+        identity = held.tile([P, P], F32, name="identity")
         hidden = [held.tile([P, N], BF16, name=f"hidden{b}") for b in blocks]
         y = [held.tile([P, N], F32, name=f"y{b}") for b in blocks]
         window = [held.tile([P, S], F32, name=f"window{b}") for b in blocks]
-        total = [held.tile([P, S], F32, name=f"total{b}") for b in blocks]
+        pos_rows = [held.tile([P, S], F32, name=f"pos_rows{b}") for b in blocks]
+        result = [held.tile([P, S], F32, name=f"result{b}") for b in blocks]
 
         nc.sync.dma_start(offsets[:], offs)
-        queues = [nc.sync, nc.scalar]
-        with nc.allow_non_contiguous_dma(reason="three bias vectors, one float32 to a partition"):
+        with nc.allow_non_contiguous_dma(reason="a bias vector, one float32 to a partition"):
             nc.sync.dma_start(b1_cols[:], b1.rearrange("(b p) o -> p (b o)", p=P))
-            nc.scalar.dma_start(b2_cols[:], b2.rearrange("(b p) o -> p (b o)", p=P))
-            nc.scalar.dma_start(tok_cols[:], tok.rearrange("(b p) o -> p (b o)", p=P))
-        for b in blocks:
-            queues[b].dma_start(w1_rows[b][:], w1[block(b), :])
-        for j in range(N // BANK):
-            for b in blocks:
-                queues[b].dma_start(table[b][:, piece(j, BANK)], prompt_table[block(b), piece(j, BANK)])
-        for b in blocks:
-            queues[b].dma_start(w2_rows[b][:], w2[block(b), :])
-        for tiles, array in ((window, base), (total, pos)):
-            for b in blocks:
-                for half in range(2):
-                    queues[half].dma_start(tiles[b][:, piece(half, S // 2)], array[block(b), piece(half, S // 2)])
+        nc.scalar.dma_start(w1_rows[:], w1.rearrange("(kb p) i -> p kb i", p=P))
+        for half in range(2):
+            cols = piece(half, N // 2)
+            nc.sync.dma_start(table[0][:, cols], prompt_table[block(0), cols])
+            nc.scalar.dma_start(table[1][:, cols], prompt_table[block(1), cols])
+        nc.scalar.dma_start(w2_rows[:], w2.rearrange("(ib p) c -> p ib c", p=P))
+        with nc.allow_non_contiguous_dma(reason="two bias vectors, one float32 to a partition"):
+            nc.sync.dma_start(b2_cols[:], b2.rearrange("(b p) o -> p (b o)", p=P))
+            nc.sync.dma_start(tok_cols[:], tok.rearrange("(b p) o -> p (b o)", p=P))
+        nc.sync.dma_start(window[0][:], base[block(0), :])
+        nc.sync.dma_start(pos_rows[0][:], pos[block(0), :])
+        nc.sync.dma_start(pos_rows[1][:], pos[block(1), :])
+        nc.sync.dma_start(window[1][:], base[block(1), :])
 
         for b in blocks:
             nc.gpsimd.tensor_copy(b2_wide[b][:], b2_cols[:, b : b + 1].to_broadcast([P, N]))
-
-        def layer1(j):
-            cols = piece(j, BANK)
-            for ib in blocks:
-                acc_h = psum_h.tile([P, BANK], F32, name="acc_h")
-                for kb in blocks:
-                    nc.tensor.matmul(
-                        acc_h[:], w1_rows[kb][:, block(ib)], table[kb][:, cols],
-                        start=(kb == 0), stop=(kb == BLOCKS - 1),
-                    )
-                if ib == 0:
-                    nc.scalar.activation(hidden[ib][:, cols], acc_h[:], ACT.Relu, bias=b1_cols[:, ib : ib + 1])
-                else:
-                    nc.vector.tensor_scalar(hidden[ib][:, cols], acc_h[:], b1_cols[:, ib : ib + 1], 0.0, ALU.add, ALU.max)
-
-        def layer2(cb, j):
-            cols = piece(j, BANK)
-            acc_y = psum_y.tile([P, BANK], F32, name="acc_y")
-            for ib in blocks:
-                nc.tensor.matmul(
-                    acc_y[:], w2_rows[ib][:, block(cb)], hidden[ib][:, cols],
-                    start=(ib == 0), stop=(ib == BLOCKS - 1),
-                )
-            if cb == 0:
-                nc.vector.tensor_copy(y[cb][:, cols], acc_y[:])
-            else:
-                nc.scalar.copy(y[cb][:, cols], acc_y[:])
+        make_identity(nc, identity[:])
 
         def scatter(cb):
             nc.vector.tensor_tensor(window[cb][:].indirect(offsets[:]), y[cb][:], b2_wide[cb][:], ALU.add)
 
-        def finish(cb, engine):
-            for i in range(S // STORE):
-                cols = piece(i, STORE)
-                engine.tensor_tensor(total[cb][:, cols], window[cb][:, cols], total[cb][:, cols], ALU.add)
-                nc.sync.dma_start(out[block(cb), cols], total[cb][:, cols])
+        with tc.psum_pool(name="psum_h", bufs=4) as psum_h, tc.psum_pool(name="psum_y", bufs=2) as psum_y:
 
-        steps = N // BANK
-        layer1(0)
-        for j in range(1, steps):
-            layer1(j)
-            layer2(0, j - 1)
-        layer2(0, steps - 1)
-        scatter(0)
-        for j in range(steps):
-            layer2(1, j)
-        scatter(1)
+            def layer1(j):
+                cols = piece(j, BANK)
+                for ib in blocks:
+                    acc_h = psum_h.tile([P, BANK], F32, name="acc_h")
+                    for kb in blocks:
+                        nc.tensor.matmul(
+                            acc_h[:], w1_rows[:, kb, block(ib)], table[kb][:, cols],
+                            start=(kb == 0), stop=(kb == BLOCKS - 1),
+                        )
+                    bias = b1_cols[:, ib : ib + 1]
+                    if ib == 0:
+                        nc.scalar.activation(hidden[ib][:, cols], acc_h[:], ACT.Relu, bias=bias)
+                    else:
+                        nc.vector.tensor_scalar(hidden[ib][:, cols], acc_h[:], bias, 0.0, ALU.add, ALU.max)
 
-        for cb in blocks:
-            nc.scalar.activation(total[cb][:], total[cb][:], ACT.Identity, bias=tok_cols[:, cb : cb + 1])
+            def layer2(cb, j):
+                cols = piece(j, BANK)
+                acc_y = psum_y.tile([P, BANK], F32, name="acc_y")
+                for ib in blocks:
+                    nc.tensor.matmul(
+                        acc_y[:], w2_rows[:, ib, block(cb)], hidden[ib][:, cols],
+                        start=(ib == 0), stop=(ib == BLOCKS - 1),
+                    )
+                if cb == 0:
+                    nc.vector.tensor_copy(y[cb][:, cols], acc_y[:])
+                else:
+                    nc.scalar.copy(y[cb][:, cols], acc_y[:])
 
-        finish(0, nc.gpsimd)
-        finish(1, nc.vector)
+            steps = N // BANK
+            layer1(0)
+            for j in range(1, steps):
+                layer1(j)
+                layer2(0, j - 1)
+            layer2(0, steps - 1)
+            scatter(0)
+            for j in range(steps):
+                layer2(1, j)
+            scatter(1)
+
+        nc.scalar.activation(result[1][:], pos_rows[1][:], ACT.Identity, bias=tok_cols[:, 1:2])
+
+        with tc.psum_pool(name="psum_sum", bufs=BANKS) as psum_sum:
+            sums = []
+            for i in range(BANKS):
+                acc_sum = psum_sum.tile([P, BANK], F32, name="acc_sum")
+                nc.tensor.matmul(acc_sum[:], identity[:], pos_rows[0][:, piece(i, BANK)], start=True, stop=False)
+                sums.append(acc_sum)
+            for i in range(BANKS):
+                cols = piece(i, BANK)
+                nc.tensor.matmul(sums[i][:], identity[:], window[0][:, cols], start=False, stop=True)
+                nc.scalar.activation(result[0][:, cols], sums[i][:], ACT.Identity, bias=tok_cols[:, 0:1])
+                nc.sync.dma_start(out[block(0), cols], result[0][:, cols])
+
+        for i in range(S // STORE):
+            cols = piece(i, STORE)
+            nc.vector.tensor_tensor(result[1][:, cols], window[1][:, cols], result[1][:, cols], ALU.add)
+            nc.sync.dma_start(out[block(1), cols], result[1][:, cols])

@@ -6,7 +6,7 @@ C, S, N = 256, 4096, 2048
 BLOCKS = C // P
 BANK = 512
 BANKS = 8
-STORE = 1024
+STORE = 512
 
 FLOPS = 2 * 2 * C * C * N
 
@@ -42,17 +42,16 @@ def tile_pclembeddings_s_kernel(tc, base, pos, tok, prompt_table, w1, b1, w2, b2
         pos_rows = [held.tile([P, S], F32, name=f"pos_rows{b}") for b in blocks]
         result = [held.tile([P, S], F32, name=f"result{b}") for b in blocks]
 
-        nc.sync.dma_start(offsets[:], offs)
-        with nc.allow_non_contiguous_dma(reason="a bias vector, one float32 to a partition"):
+        with nc.allow_non_contiguous_dma(reason="two bias vectors, one float32 to a partition"):
             nc.sync.dma_start(b1_cols[:], b1.rearrange("(b p) o -> p (b o)", p=P))
+            nc.sync.dma_start(b2_cols[:], b2.rearrange("(b p) o -> p (b o)", p=P))
         nc.scalar.dma_start(w1_rows[:], w1.rearrange("(kb p) i -> p kb i", p=P))
-        for half in range(2):
-            cols = piece(half, N // 2)
+        for cols in (slice(0, BANK), slice(BANK, N)):
             nc.sync.dma_start(table[0][:, cols], prompt_table[block(0), cols])
             nc.scalar.dma_start(table[1][:, cols], prompt_table[block(1), cols])
         nc.scalar.dma_start(w2_rows[:], w2.rearrange("(ib p) c -> p ib c", p=P))
-        with nc.allow_non_contiguous_dma(reason="two bias vectors, one float32 to a partition"):
-            nc.sync.dma_start(b2_cols[:], b2.rearrange("(b p) o -> p (b o)", p=P))
+        nc.sync.dma_start(offsets[:], offs)
+        with nc.allow_non_contiguous_dma(reason="a bias vector, one float32 to a partition"):
             nc.sync.dma_start(tok_cols[:], tok.rearrange("(b p) o -> p (b o)", p=P))
         nc.sync.dma_start(window[0][:], base[block(0), :])
         nc.sync.dma_start(pos_rows[0][:], pos[block(0), :])

@@ -7,6 +7,7 @@ BLOCKS = C // P
 BANK = 512
 BANKS = 8
 STORE = 512
+WARM_UP = 6
 
 FLOPS = 2 * 2 * C * C * N
 
@@ -65,7 +66,16 @@ def tile_pclembeddings_s_kernel(tc, base, pos, tok, prompt_table, w1, b1, w2, b2
         def scatter(cb):
             nc.vector.tensor_tensor(window[cb][:].indirect(offsets[:]), y[cb][:], b2_wide[cb][:], ALU.add)
 
-        with tc.psum_pool(name="psum_h", bufs=4) as psum_h, tc.psum_pool(name="psum_y", bufs=2) as psum_y:
+        with (
+            tc.psum_pool(name="psum_h", bufs=4) as psum_h,
+            tc.psum_pool(name="psum_y", bufs=2) as psum_y,
+            tc.psum_pool(name="psum_idle", bufs=1) as psum_idle,
+        ):
+            zeros = held.tile([P, BANK], BF16, name="zeros")
+            nc.vector.memset(zeros[:], 0.0)
+            unread = psum_idle.tile([P, BANK], F32, name="unread")
+            for repeat in range(WARM_UP):
+                nc.tensor.matmul(unread[:], zeros[:, 0:P], zeros[:], start=True, stop=True)
 
             def layer1(j):
                 cols = piece(j, BANK)

@@ -7,7 +7,6 @@ BLOCKS = C // P
 BANK = 512
 BANKS = 8
 STORE = 512
-WARM_UP = 6
 
 FLOPS = 2 * 2 * C * C * N
 
@@ -56,8 +55,8 @@ def tile_pclembeddings_s_kernel(tc, base, pos, tok, prompt_table, w1, b1, w2, b2
             nc.sync.dma_start(tok_cols[:], tok.rearrange("(b p) o -> p (b o)", p=P))
         nc.sync.dma_start(window[0][:], base[block(0), :])
         nc.sync.dma_start(pos_rows[0][:], pos[block(0), :])
-        nc.sync.dma_start(pos_rows[1][:], pos[block(1), :])
         nc.sync.dma_start(window[1][:], base[block(1), :])
+        nc.sync.dma_start(pos_rows[1][:], pos[block(1), :])
 
         for b in blocks:
             nc.gpsimd.tensor_copy(b2_wide[b][:], b2_cols[:, b : b + 1].to_broadcast([P, N]))
@@ -66,16 +65,7 @@ def tile_pclembeddings_s_kernel(tc, base, pos, tok, prompt_table, w1, b1, w2, b2
         def scatter(cb):
             nc.vector.tensor_tensor(window[cb][:].indirect(offsets[:]), y[cb][:], b2_wide[cb][:], ALU.add)
 
-        with (
-            tc.psum_pool(name="psum_h", bufs=4) as psum_h,
-            tc.psum_pool(name="psum_y", bufs=2) as psum_y,
-            tc.psum_pool(name="psum_idle", bufs=1) as psum_idle,
-        ):
-            zeros = held.tile([P, BANK], BF16, name="zeros")
-            nc.vector.memset(zeros[:], 0.0)
-            unread = psum_idle.tile([P, BANK], F32, name="unread")
-            for repeat in range(WARM_UP):
-                nc.tensor.matmul(unread[:], zeros[:, 0:P], zeros[:], start=True, stop=True)
+        with tc.psum_pool(name="psum_h", bufs=4) as psum_h, tc.psum_pool(name="psum_y", bufs=2) as psum_y:
 
             def layer1(j):
                 cols = piece(j, BANK)
@@ -116,8 +106,6 @@ def tile_pclembeddings_s_kernel(tc, base, pos, tok, prompt_table, w1, b1, w2, b2
                 layer2(1, j)
             scatter(1)
 
-        nc.scalar.activation(result[1][:], pos_rows[1][:], ACT.Identity, bias=tok_cols[:, 1:2])
-
         with tc.psum_pool(name="psum_sum", bufs=BANKS) as psum_sum:
             sums = []
             for i in range(BANKS):
@@ -132,5 +120,7 @@ def tile_pclembeddings_s_kernel(tc, base, pos, tok, prompt_table, w1, b1, w2, b2
 
         for i in range(S // STORE):
             cols = piece(i, STORE)
-            nc.vector.tensor_tensor(result[1][:, cols], window[1][:, cols], result[1][:, cols], ALU.add)
+            nc.vector.scalar_tensor_tensor(
+                result[1][:, cols], window[1][:, cols], tok_cols[:, 1:2], pos_rows[1][:, cols], ALU.add, ALU.add
+            )
             nc.sync.dma_start(out[block(1), cols], result[1][:, cols])

@@ -106,6 +106,8 @@ def tile_pclembeddings_s_kernel(tc, base, pos, tok, prompt_table, w1, b1, w2, b2
                 layer2(1, j)
             scatter(1)
 
+        nc.scalar.activation(result[1][:], pos_rows[1][:], ACT.Identity, bias=tok_cols[:, 1:2])
+
         with tc.psum_pool(name="psum_sum", bufs=BANKS) as psum_sum:
             sums = []
             for i in range(BANKS):
@@ -120,7 +122,5 @@ def tile_pclembeddings_s_kernel(tc, base, pos, tok, prompt_table, w1, b1, w2, b2
 
         for i in range(S // STORE):
             cols = piece(i, STORE)
-            nc.vector.scalar_tensor_tensor(
-                result[1][:, cols], window[1][:, cols], tok_cols[:, 1:2], pos_rows[1][:, cols], ALU.add, ALU.add
-            )
+            nc.vector.tensor_tensor(result[1][:, cols], window[1][:, cols], result[1][:, cols], ALU.add)
             nc.sync.dma_start(out[block(1), cols], result[1][:, cols])

@@ -42,18 +42,19 @@ def tile_pclembeddings_s_kernel(tc, base, pos, tok, prompt_table, w1, b1, w2, b2
         pos_rows = [held.tile([P, S], F32, name=f"pos_rows{b}") for b in blocks]
         result = [held.tile([P, S], F32, name=f"result{b}") for b in blocks]
 
-        with nc.allow_non_contiguous_dma(reason="two bias vectors, one float32 to a partition"):
-            nc.sync.dma_start(b1_cols[:], b1.rearrange("(b p) o -> p (b o)", p=P))
-            nc.sync.dma_start(b2_cols[:], b2.rearrange("(b p) o -> p (b o)", p=P))
         nc.scalar.dma_start(w1_rows[:], w1.rearrange("(kb p) i -> p kb i", p=P))
-        for cols in (slice(0, BANK), slice(BANK, N)):
-            nc.sync.dma_start(table[0][:, cols], prompt_table[block(0), cols])
-            nc.scalar.dma_start(table[1][:, cols], prompt_table[block(1), cols])
-        nc.scalar.dma_start(w2_rows[:], w2.rearrange("(ib p) c -> p ib c", p=P))
-        nc.sync.dma_start(offsets[:], offs)
+        nc.sync.dma_start(table[0][:, 0:BANK], prompt_table[block(0), 0:BANK])
+        nc.scalar.dma_start(table[1][:, 0:BANK], prompt_table[block(1), 0:BANK])
         with nc.allow_non_contiguous_dma(reason="a bias vector, one float32 to a partition"):
-            nc.sync.dma_start(tok_cols[:], tok.rearrange("(b p) o -> p (b o)", p=P))
+            nc.sync.dma_start(b1_cols[:], b1.rearrange("(b p) o -> p (b o)", p=P))
+        nc.sync.dma_start(table[0][:, BANK:N], prompt_table[block(0), BANK:N])
+        nc.scalar.dma_start(table[1][:, BANK:N], prompt_table[block(1), BANK:N])
+        nc.scalar.dma_start(w2_rows[:], w2.rearrange("(ib p) c -> p ib c", p=P))
+        with nc.allow_non_contiguous_dma(reason="two bias vectors, one float32 to a partition"):
+            nc.scalar.dma_start(b2_cols[:], b2.rearrange("(b p) o -> p (b o)", p=P))
+            nc.scalar.dma_start(tok_cols[:], tok.rearrange("(b p) o -> p (b o)", p=P))
         nc.sync.dma_start(window[0][:], base[block(0), :])
+        nc.sync.dma_start(offsets[:], offs)
         nc.sync.dma_start(pos_rows[0][:], pos[block(0), :])
         nc.sync.dma_start(window[1][:], base[block(1), :])
         nc.sync.dma_start(pos_rows[1][:], pos[block(1), :])

@@ -45,16 +45,16 @@ def tile_pclembeddings_s_kernel(tc, base, pos, tok, prompt_table, w1, b1, w2, b2
         nc.scalar.dma_start(w1_rows[:], w1.rearrange("(kb p) i -> p kb i", p=P))
         nc.sync.dma_start(table[0][:, 0:BANK], prompt_table[block(0), 0:BANK])
         nc.scalar.dma_start(table[1][:, 0:BANK], prompt_table[block(1), 0:BANK])
-        with nc.allow_non_contiguous_dma(reason="a bias vector, one float32 to a partition"):
+        with nc.allow_non_contiguous_dma(reason="two bias vectors, one float32 to a partition"):
             nc.sync.dma_start(b1_cols[:], b1.rearrange("(b p) o -> p (b o)", p=P))
+            nc.sync.dma_start(b2_cols[:], b2.rearrange("(b p) o -> p (b o)", p=P))
         nc.sync.dma_start(table[0][:, BANK:N], prompt_table[block(0), BANK:N])
         nc.scalar.dma_start(table[1][:, BANK:N], prompt_table[block(1), BANK:N])
         nc.scalar.dma_start(w2_rows[:], w2.rearrange("(ib p) c -> p ib c", p=P))
-        with nc.allow_non_contiguous_dma(reason="two bias vectors, one float32 to a partition"):
-            nc.scalar.dma_start(b2_cols[:], b2.rearrange("(b p) o -> p (b o)", p=P))
-            nc.scalar.dma_start(tok_cols[:], tok.rearrange("(b p) o -> p (b o)", p=P))
-        nc.sync.dma_start(window[0][:], base[block(0), :])
         nc.sync.dma_start(offsets[:], offs)
+        with nc.allow_non_contiguous_dma(reason="a bias vector, one float32 to a partition"):
+            nc.sync.dma_start(tok_cols[:], tok.rearrange("(b p) o -> p (b o)", p=P))
+        nc.sync.dma_start(window[0][:], base[block(0), :])
         nc.sync.dma_start(pos_rows[0][:], pos[block(0), :])
         nc.sync.dma_start(window[1][:], base[block(1), :])
         nc.sync.dma_start(pos_rows[1][:], pos[block(1), :])

@@ -59,9 +59,8 @@ def tile_pclembeddings_s_kernel(tc, base, pos, tok, prompt_table, w1, b1, w2, b2
         nc.sync.dma_start(window[1][:], base[block(1), :])
         nc.sync.dma_start(pos_rows[1][:], pos[block(1), :])
 
-        for b in blocks:
-            nc.gpsimd.tensor_copy(b2_wide[b][:], b2_cols[:, b : b + 1].to_broadcast([P, N]))
         make_identity(nc, identity[:])
+        nc.vector.tensor_copy(b2_wide[0][:], b2_cols[:, 0:1].to_broadcast([P, N]))
 
         def scatter(cb):
             nc.vector.tensor_tensor(window[cb][:].indirect(offsets[:]), y[cb][:], b2_wide[cb][:], ALU.add)
@@ -103,6 +102,7 @@ def tile_pclembeddings_s_kernel(tc, base, pos, tok, prompt_table, w1, b1, w2, b2
                 layer2(0, j - 1)
             layer2(0, steps - 1)
             scatter(0)
+            nc.scalar.copy(b2_wide[1][:], b2_cols[:, 1:2].to_broadcast([P, N]))
             for j in range(steps):
                 layer2(1, j)
             scatter(1)

@@ -65,7 +65,7 @@ def tile_pclembeddings_s_kernel(tc, base, pos, tok, prompt_table, w1, b1, w2, b2
         def scatter(cb):
             nc.vector.tensor_tensor(window[cb][:].indirect(offsets[:]), y[cb][:], b2_wide[cb][:], ALU.add)
 
-        with tc.psum_pool(name="psum_h", bufs=4) as psum_h, tc.psum_pool(name="psum_y", bufs=2) as psum_y:
+        with tc.psum_pool(name="psum_h", bufs=4) as psum_h, tc.psum_pool(name="psum_y", bufs=4) as psum_y:
 
             def layer1(j):
                 cols = piece(j, BANK)
@@ -90,17 +90,16 @@ def tile_pclembeddings_s_kernel(tc, base, pos, tok, prompt_table, w1, b1, w2, b2
                         acc_y[:], w2_rows[:, ib, block(cb)], hidden[ib][:, cols],
                         start=(ib == 0), stop=(ib == BLOCKS - 1),
                     )
-                if cb == 0:
+                if cb == 0 and j % 2 == 0:
                     nc.vector.tensor_copy(y[cb][:, cols], acc_y[:])
                 else:
                     nc.scalar.copy(y[cb][:, cols], acc_y[:])
 
             steps = N // BANK
-            layer1(0)
-            for j in range(1, steps):
+            for j in range(steps):
                 layer1(j)
-                layer2(0, j - 1)
-            layer2(0, steps - 1)
+            for j in range(steps):
+                layer2(0, j)
             scatter(0)
             nc.scalar.copy(b2_wide[1][:], b2_cols[:, 1:2].to_broadcast([P, N]))
             for j in range(steps):

@@ -82,28 +82,30 @@ def tile_pclembeddings_s_kernel(tc, base, pos, tok, prompt_table, w1, b1, w2, b2
                     else:
                         nc.vector.tensor_scalar(hidden[ib][:, cols], acc_h[:], bias, 0.0, ALU.add, ALU.max)
 
-            def layer2(cb, j):
-                cols = piece(j, BANK)
+            def layer2(cb, first, width, turn):
+                cols = slice(first, first + width)
                 acc_y = psum_y.tile([P, BANK], F32, name="acc_y")
                 for ib in blocks:
                     nc.tensor.matmul(
-                        acc_y[:], w2_rows[:, ib, block(cb)], hidden[ib][:, cols],
+                        acc_y[:, 0:width], w2_rows[:, ib, block(cb)], hidden[ib][:, cols],
                         start=(ib == 0), stop=(ib == BLOCKS - 1),
                     )
-                if cb == 0 and j % 2 == 0:
-                    nc.vector.tensor_copy(y[cb][:, cols], acc_y[:])
+                if cb == 0 and turn % 2 == 0:
+                    nc.vector.tensor_copy(y[cb][:, cols], acc_y[:, 0:width])
                 else:
-                    nc.scalar.copy(y[cb][:, cols], acc_y[:])
+                    nc.scalar.copy(y[cb][:, cols], acc_y[:, 0:width])
 
             steps = N // BANK
             for j in range(steps):
                 layer1(j)
-            for j in range(steps):
-                layer2(0, j)
+            for j in range(steps - 1):
+                layer2(0, j * BANK, BANK, j)
+            layer2(0, N - BANK, BANK // 2, steps - 1)
+            layer2(0, N - BANK // 2, BANK // 2, steps)
             scatter(0)
             nc.scalar.copy(b2_wide[1][:], b2_cols[:, 1:2].to_broadcast([P, N]))
             for j in range(steps):
-                layer2(1, j)
+                layer2(1, j * BANK, BANK, j)
             scatter(1)
 
         nc.scalar.activation(result[1][:], pos_rows[1][:], ACT.Identity, bias=tok_cols[:, 1:2])

import concourse.mybir as mybir
from concourse.masks import make_identity

P = 128
C, S, N = 256, 4096, 2048
BLOCKS = C // P
BANK = 512
BANKS = 8
STORE = 512

FLOPS = 2 * 2 * C * C * N

F32, BF16, U16 = mybir.dt.float32, mybir.dt.bfloat16, mybir.dt.uint16
ALU = mybir.AluOpType
ACT = mybir.ActivationFunctionType


def block(b):
    return slice(b * P, (b + 1) * P)


def piece(i, width):
    return slice(i * width, (i + 1) * width)


def tile_pclembeddings_s_kernel(tc, base, pos, tok, prompt_table, w1, b1, w2, b2, offs, out):
    nc = tc.nc
    blocks = range(BLOCKS)
    with tc.tile_pool(name="held", bufs=1) as held:
        offsets = held.tile([P, N // 16], U16, name="offsets")
        w1_rows = held.tile([P, BLOCKS, C], BF16, name="w1_rows")
        w2_rows = held.tile([P, BLOCKS, C], BF16, name="w2_rows")
        table = [held.tile([P, N], BF16, name=f"table{b}") for b in blocks]
        b1_cols = held.tile([P, BLOCKS], F32, name="b1_cols")
        b2_cols = held.tile([P, BLOCKS], F32, name="b2_cols")
        tok_cols = held.tile([P, BLOCKS], F32, name="tok_cols")
        b2_wide = [held.tile([P, N], F32, name=f"b2_wide{b}") for b in blocks]
        identity = held.tile([P, P], F32, name="identity")
        hidden = [held.tile([P, N], BF16, name=f"hidden{b}") for b in blocks]
        y = [held.tile([P, N], F32, name=f"y{b}") for b in blocks]
        window = [held.tile([P, S], F32, name=f"window{b}") for b in blocks]
        pos_rows = [held.tile([P, S], F32, name=f"pos_rows{b}") for b in blocks]
        result = [held.tile([P, S], F32, name=f"result{b}") for b in blocks]

        nc.scalar.dma_start(w1_rows[:], w1.rearrange("(kb p) i -> p kb i", p=P))
        nc.sync.dma_start(table[0][:, 0:BANK], prompt_table[block(0), 0:BANK])
        nc.scalar.dma_start(table[1][:, 0:BANK], prompt_table[block(1), 0:BANK])
        with nc.allow_non_contiguous_dma(reason="two bias vectors, one float32 to a partition"):
            nc.sync.dma_start(b1_cols[:], b1.rearrange("(b p) o -> p (b o)", p=P))
            nc.sync.dma_start(b2_cols[:], b2.rearrange("(b p) o -> p (b o)", p=P))
        nc.sync.dma_start(table[0][:, BANK:N], prompt_table[block(0), BANK:N])
        nc.scalar.dma_start(table[1][:, BANK:N], prompt_table[block(1), BANK:N])
        nc.scalar.dma_start(w2_rows[:], w2.rearrange("(ib p) c -> p ib c", p=P))
        nc.sync.dma_start(offsets[:], offs)
        with nc.allow_non_contiguous_dma(reason="a bias vector, one float32 to a partition"):
            nc.sync.dma_start(tok_cols[:], tok.rearrange("(b p) o -> p (b o)", p=P))
        nc.sync.dma_start(window[0][:], base[block(0), :])
        nc.sync.dma_start(pos_rows[0][:], pos[block(0), :])
        nc.sync.dma_start(window[1][:], base[block(1), :])
        nc.sync.dma_start(pos_rows[1][:], pos[block(1), :])

        make_identity(nc, identity[:])
        nc.vector.tensor_copy(b2_wide[0][:], b2_cols[:, 0:1].to_broadcast([P, N]))

        def scatter(cb):
            nc.vector.tensor_tensor(window[cb][:].indirect(offsets[:]), y[cb][:], b2_wide[cb][:], ALU.add)

        with tc.psum_pool(name="psum_h", bufs=4) as psum_h, tc.psum_pool(name="psum_y", bufs=4) as psum_y:

            def layer1(j):
                cols = piece(j, BANK)
                for ib in blocks:
                    acc_h = psum_h.tile([P, BANK], F32, name="acc_h")
                    for kb in blocks:
                        nc.tensor.matmul(
                            acc_h[:], w1_rows[:, kb, block(ib)], table[kb][:, cols],
                            start=(kb == 0), stop=(kb == BLOCKS - 1),
                        )
                    bias = b1_cols[:, ib : ib + 1]
                    if ib == 0:
                        nc.scalar.activation(hidden[ib][:, cols], acc_h[:], ACT.Relu, bias=bias)
                    else:
                        nc.vector.tensor_scalar(hidden[ib][:, cols], acc_h[:], bias, 0.0, ALU.add, ALU.max)

            def layer2(cb, first, width, turn):
                cols = slice(first, first + width)
                acc_y = psum_y.tile([P, BANK], F32, name="acc_y")
                for ib in blocks:
                    nc.tensor.matmul(
                        acc_y[:, 0:width], w2_rows[:, ib, block(cb)], hidden[ib][:, cols],
                        start=(ib == 0), stop=(ib == BLOCKS - 1),
                    )
                if cb == 0 and turn % 2 == 0:
                    nc.vector.tensor_copy(y[cb][:, cols], acc_y[:, 0:width])
                else:
                    nc.scalar.copy(y[cb][:, cols], acc_y[:, 0:width])

            steps = N // BANK
            for j in range(steps):
                layer1(j)
            for j in range(steps - 1):
                layer2(0, j * BANK, BANK, j)
            layer2(0, N - BANK, BANK // 2, steps - 1)
            layer2(0, N - BANK // 2, BANK // 2, steps)
            scatter(0)
            nc.scalar.copy(b2_wide[1][:], b2_cols[:, 1:2].to_broadcast([P, N]))
            for j in range(steps):
                layer2(1, j * BANK, BANK, j)
            scatter(1)

        nc.scalar.activation(result[1][:], pos_rows[1][:], ACT.Identity, bias=tok_cols[:, 1:2])

        with tc.psum_pool(name="psum_sum", bufs=BANKS) as psum_sum:
            sums = []
            for i in range(BANKS):
                acc_sum = psum_sum.tile([P, BANK], F32, name="acc_sum")
                nc.tensor.matmul(acc_sum[:], identity[:], pos_rows[0][:, piece(i, BANK)], start=True, stop=False)
                sums.append(acc_sum)
            for i in range(BANKS):
                cols = piece(i, BANK)
                nc.tensor.matmul(sums[i][:], identity[:], window[0][:, cols], start=False, stop=True)
                nc.scalar.activation(result[0][:, cols], sums[i][:], ACT.Identity, bias=tok_cols[:, 0:1])
                nc.sync.dma_start(out[block(0), cols], result[0][:, cols])

        for i in range(S // STORE):
            cols = piece(i, STORE)
            nc.vector.tensor_tensor(result[1][:, cols], window[1][:, cols], result[1][:, cols], ALU.add)
            nc.sync.dma_start(out[block(1), cols], result[1][:, cols])
